import numpy as np
import ml_dtypes


def mxq(x, axis, fmt="e4m3"):
    dtype, down = {"e4m3": (ml_dtypes.float8_e4m3fn, 7), "e5m2": (ml_dtypes.float8_e5m2, 14)}[fmt]
    v = np.moveaxis(np.asarray(x, np.float32).astype(ml_dtypes.bfloat16).astype(np.float64), axis, -1)
    blocks = v.reshape(v.shape[:-1] + (-1, 32))
    amax = np.abs(blocks).max(-1, keepdims=True)
    byte = np.maximum(np.where(amax > 0, np.frexp(amax)[1] - 1 + 127, 0) - down, 1)
    scale = np.exp2(byte - 127.0)
    codes = (blocks / scale).astype(np.float32).astype(dtype).astype(np.float64)
    return np.moveaxis((codes * scale).reshape(v.shape), -1, axis)


WIDE = False


def mx_kscale(k):
    if not WIDE:
        return np.ones(k)
    levels = np.array([10, -10, 5, -5, 0])
    a = np.random.permutation(np.resize(levels, k // 512 * 4)).reshape(k // 512, 4)
    idx = np.arange(k)
    return np.exp2(a[idx // 512, idx % 128 // 32])


BF16 = ml_dtypes.bfloat16


def bf(x):
    return np.asarray(x, np.float32).astype(BF16)


def f64(x):
    return np.asarray(x).astype(np.float64)


E2M1 = np.array([0.0, 0.5, 1.0, 1.5, 2.0, 3.0, 4.0, 6.0, -0.0, -0.5, -1.0, -1.5, -2.0, -3.0, -4.0, -6.0])


def pack_weight(w, fmt):
    k, n = w.shape
    w = f64(bf(w)).reshape(k // 32, 32, n)
    amax = np.abs(w).max(1)
    if fmt == "e4m3":
        byte = np.frexp(amax)[1] - 1 + 127 - 7
    else:
        mant, ex = np.frexp(amax / 6.0)
        byte = np.where(mant > 0.5, ex, ex - 1) + 127
    byte = np.clip(np.where(amax > 0, byte, 1), 1, 254)
    scaled = (w * np.exp2(127.0 - byte)[:, None, :]).reshape(k, n).astype(np.float32)
    by_word = np.ascontiguousarray(scaled.reshape(k // 512, 128, 4, n).transpose(0, 1, 3, 2))
    if fmt == "e4m3":
        words = by_word.astype(ml_dtypes.float8_e4m3fn).view(np.uint8)
    else:
        c = by_word.astype(ml_dtypes.float4_e2m1fn).view(np.uint8) & 0xF
        words = c[..., 0::2] | (c[..., 1::2] << 4)
    return np.ascontiguousarray(words), np.ascontiguousarray(byte.astype(np.uint8).reshape(k // 512, 16, n))


def unpack_weight(words, scales, fmt):
    g, p, n, _ = words.shape
    if fmt == "e4m3":
        vals = np.ascontiguousarray(words).view(ml_dtypes.float8_e4m3fn).astype(np.float64)
    else:
        nib = np.empty((g, p, n, 4), np.uint8)
        nib[..., 0::2] = words & 0xF
        nib[..., 1::2] = words >> 4
        vals = E2M1[nib]
    vals = vals * np.repeat(np.exp2(scales.astype(np.float64) - 127.0), 8, axis=1)[..., None]
    return vals.transpose(0, 1, 3, 2).reshape(g * 512, n)


B, N, F, G, K = 64, 128, 512, 512, 2048
EPS = 1e-8


def setup_inputs():
    s = mx_kscale(F)
    a = np.random.standard_normal((B, N, 1))
    g = np.random.standard_normal((B, 1, F))
    h = 2.0 * (np.random.standard_normal((B, N, F)) + a * g)
    w = (np.random.standard_normal((F, G)) + 0.5 * np.random.standard_normal((F, 1))) / np.sqrt(F)
    words, scales = pack_weight(w / s[:, None], "e4m3")
    return {"h": bf(h * s), "W_h_words": words, "W_h_scales": scales, "beta": bf(2.0 + np.random.uniform(size=1))}


def reference(h, W_h_words, W_h_scales, beta):
    Wh = mxq(f64(h), 2, "e4m3") @ unpack_weight(W_h_words, W_h_scales, "e4m3")
    xm = Wh - Wh.mean(-1, keepdims=True)
    xq = mxq(xm, 2, "e4m3")
    cov = xq @ xq.transpose(0, 2, 1)
    norm = np.sqrt((xm * xm).sum(-1))
    denom = norm[:, :, None] * norm[:, None, :] + EPS
    return f64(beta) * np.abs(cov / denom)

@@ -1,0 +1,229 @@
+from contextlib import ExitStack
+
+import concourse.mybir as mybir
+from concourse.masks import make_identity
+
+F32 = mybir.dt.float32
+BF16 = mybir.dt.bfloat16
+I32 = mybir.dt.int32
+U32 = mybir.dt.uint32
+U8 = mybir.dt.uint8
+FP8X4 = mybir.dt.float8_e4m3fn_x4
+ACT = mybir.ActivationFunctionType
+ALU = mybir.AluOpType
+
+P = 128
+GRAPHS = 64
+NODES = 128
+F_IN = 512
+F_OUT = 512
+HALVES = 2
+PAIR = 2
+PAIRS = GRAPHS // PAIR
+EPS = 1e-8
+TINY = 1e-36
+
+FLOPS = 2 * GRAPHS * NODES * F_IN * F_OUT + 2 * GRAPHS * NODES * NODES * F_OUT
+
+
+def tile_pearsonattention_pa_t_kernel(tc, h, W_h_words, W_h_scales, beta, out):
+    nc = tc.nc
+    with ExitStack() as ctx:
+        const = ctx.enter_context(tc.tile_pool(name="const", bufs=1))
+        h_pool = ctx.enter_context(tc.tile_pool(name="h_pool", bufs=PAIRS))
+        work = ctx.enter_context(tc.tile_pool(name="work", bufs=3))
+        stat = ctx.enter_context(tc.tile_pool(name="stat", bufs=8))
+        res_pool = ctx.enter_context(tc.tile_pool(name="res_pool", bufs=6))
+        psum_ht = ctx.enter_context(tc.psum_pool(name="psum_ht", bufs=1))
+        psum_xt = ctx.enter_context(tc.psum_pool(name="psum_xt", bufs=1))
+        psum_wh = ctx.enter_context(tc.psum_pool(name="psum_wh", bufs=2 * PAIR))
+        psum_epi = ctx.enter_context(tc.psum_pool(name="psum_epi", bufs=2))
+
+        eps = const.tile([P, 1], F32)
+        nc.vector.memset(eps[:], EPS)
+        tiny = const.tile([P, 1], F32)
+        nc.vector.memset(tiny[:], TINY)
+        warm = const.tile([P, 1], F32)
+        nc.scalar.activation(out=warm[:], in_=eps[:], func=ACT.Abs_reciprocal_sqrt)
+
+        ident = const.tile([P, P], F32)
+        make_identity(nc, ident[:])
+
+        w_scales = const.tile([P, F_OUT], U8, align_bytes=64)
+        nc.vector.memset(w_scales[:].bitcast(I32), 0)
+        w_codes = const.tile([P, F_OUT], U32, align_bytes=64)
+        beta_bf16 = const.tile([P, 1], BF16)
+        beta_f32 = const.tile([P, 1], F32)
+
+        h_pairs = {}
+
+        def load_h(pair):
+            h_pair = h_pool.tile([P, PAIR, F_IN], BF16)
+            graphs = h[PAIR * pair : PAIR * (pair + 1)]
+            nc.sync.dma_start(out=h_pair[:], in_=graphs.rearrange("b n f -> n b f"))
+            h_pairs[pair] = h_pair
+
+        load_h(0)
+        for quadrant in range(4):
+            nc.sync.dma_start(
+                out=w_scales[32 * quadrant : 32 * quadrant + 4, :].bitcast(I32),
+                in_=W_h_scales[0, 4 * quadrant : 4 * quadrant + 4, :].bitcast(I32),
+            )
+        nc.sync.dma_start(
+            out=w_codes[:].bitcast(I32),
+            in_=W_h_words[0].rearrange("p n t -> p (n t)").bitcast(I32),
+        )
+        nc.sync.dma_start(out=beta_bf16[:], in_=beta.partition_broadcast(P))
+        for pair in range(1, PAIRS):
+            load_h(pair)
+        nc.vector.tensor_copy(out=beta_f32[:], in_=beta_bf16[:])
+
+        h_t, h_q, wh, neg_means, norms, x_m, x_t, x_q, epi = {}, {}, {}, {}, {}, {}, {}, {}, {}
+
+        def regroup(engine_copy, transposed, kind):
+            grouped = work.tile([P, PAIR * NODES * 2 * HALVES], BF16, align_bytes=64, name=kind + "_grouped")
+            engine_copy(
+                out=grouped[:].bitcast(F32).rearrange("p (g n u) -> p g n u", g=PAIR, u=HALVES),
+                in_=transposed[:].rearrange("p g u n -> p g n u"),
+            )
+            return grouped
+
+        def quantise(grouped, kind):
+            codes = work.tile([P, PAIR * NODES], U32, align_bytes=64, name=kind + "_codes")
+            scales = work.tile([P, PAIR * NODES], U8, align_bytes=64, name=kind + "_scales")
+            nc.vector.quantize_mx(out=codes[:].bitcast(FP8X4), scales=scales[:], in_=grouped[:])
+            return codes, scales
+
+        def transpose_h(pair):
+            transposed = psum_ht.tile([P, PAIR, HALVES, NODES], F32, name="h_transposed")
+            for g in range(PAIR):
+                words = h_pairs[pair][:, g, :].bitcast(F32)
+                for u in range(HALVES):
+                    nc.tensor.transpose(transposed[:, g, u, :], words[:, u : F_IN // 2 : HALVES], ident[:])
+            h_t[pair] = transposed
+
+        def quantise_h(pair):
+            h_q[pair] = quantise(regroup(nc.scalar.copy, h_t[pair], "h"), "h")
+
+        def project(pair):
+            codes, scales = h_q[pair]
+            for g in range(PAIR):
+                nodes = slice(NODES * g, NODES * (g + 1))
+                acc = psum_wh.tile([P, F_OUT], F32, name="wh_acc")
+                nc.tensor.matmul_mx(
+                    out=acc[:],
+                    lhsT=codes[:, nodes].bitcast(FP8X4),
+                    lhsT_scale=scales[:, nodes],
+                    rhs=w_codes[:].bitcast(FP8X4),
+                    rhs_scale=w_scales[:],
+                    start=True,
+                    stop=True,
+                )
+                wh[(pair, g)] = acc
+
+        def take_moments(pair):
+            mean_var = stat.tile([P, PAIR, 2], F32, name="mean_var")
+            for g in range(PAIR):
+                partial = stat.tile([P, 6], F32, name="partial")
+                nc.vector.bn_stats(out=partial[:], in_=wh[(pair, g)][:])
+                nc.vector.bn_aggr(out=mean_var[:, g, :], in_=partial[:])
+            neg_mean = stat.tile([P, PAIR], F32, name="neg_mean")
+            nc.vector.tensor_scalar_mul(out=neg_mean[:], in0=mean_var[:, :, 0], scalar1=-1.0)
+            inv_norm = stat.tile([P, PAIR], F32, name="inv_norm")
+            nc.scalar.activation(
+                out=inv_norm[:], in_=mean_var[:, :, 1], func=ACT.Abs_reciprocal_sqrt,
+                bias=tiny[:], scale=float(F_OUT),
+            )
+            norm = stat.tile([P, PAIR], F32, name="norm")
+            nc.vector.scalar_tensor_tensor(
+                out=norm[:], in0=mean_var[:, :, 1], scalar=float(F_OUT), in1=inv_norm[:],
+                op0=ALU.mult, op1=ALU.mult,
+            )
+            neg_means[pair] = neg_mean
+            norms[pair] = norm
+
+        def centre(pair):
+            neg_mean = neg_means[pair]
+            centred = work.tile([P, PAIR, F_OUT], BF16, name="centred")
+            for g in range(PAIR):
+                nc.scalar.activation(
+                    out=centred[:, g, :].rearrange("n (u p e) -> n u p e", u=HALVES, e=2),
+                    in_=wh[(pair, g)][:].rearrange("n (p u e) -> n u p e", u=HALVES, e=2),
+                    func=ACT.Identity,
+                    bias=neg_mean[:, g : g + 1],
+                    scale=1.0,
+                )
+            x_m[pair] = centred
+
+        def transpose_x(pair):
+            transposed = psum_xt.tile([P, PAIR, HALVES, NODES], F32, name="x_transposed")
+            for g in range(PAIR):
+                words = x_m[pair][:, g, :].bitcast(F32)
+                for u in range(HALVES):
+                    nc.tensor.transpose(transposed[:, g, u, :], words[:, P * u : P * (u + 1)], ident[:])
+            x_t[pair] = transposed
+
+        def quantise_x(pair):
+            x_q[pair] = quantise(regroup(nc.vector.tensor_copy, x_t[pair], "x"), "x")
+
+        def spread_norm(pair):
+            norm = norms[pair]
+            bank = psum_epi.tile([P, 2, PAIR, NODES], F32, name="epi_bank")
+            for g in range(PAIR):
+                nc.tensor.transpose(bank[:, 0, g, :], norm[:, g : g + 1].to_broadcast([P, P]), ident[:])
+            epi[pair] = bank
+
+        def correlate(pair):
+            codes, scales = x_q[pair]
+            for g in range(PAIR):
+                nodes = slice(NODES * g, NODES * (g + 1))
+                nc.tensor.matmul_mx(
+                    out=epi[pair][:, 1, g, :],
+                    lhsT=codes[:, nodes].bitcast(FP8X4),
+                    lhsT_scale=scales[:, nodes],
+                    rhs=codes[:, nodes].bitcast(FP8X4),
+                    rhs_scale=scales[:, nodes],
+                    start=True,
+                    stop=True,
+                )
+
+        def normalise(pair):
+            norm = norms[pair]
+            bank = epi[pair]
+            root = work.tile([P, PAIR, NODES], F32, name="root")
+            for g in range(PAIR):
+                nc.scalar.activation(
+                    out=root[:, g, :], in_=bank[:, 0, g, :], func=ACT.Abs_reciprocal_sqrt,
+                    bias=eps[:], scale=norm[:, g : g + 1],
+                )
+            inv_denom = work.tile([P, PAIR, NODES], F32, name="inv_denom")
+            nc.scalar.square(out=inv_denom[:], in_=root[:])
+            abs_cov = work.tile([P, PAIR, NODES], F32, name="abs_cov")
+            nc.scalar.activation(out=abs_cov[:], in_=bank[:, 1, :, :], func=ACT.Abs)
+            result = res_pool.tile([P, PAIR, NODES], F32, name="result")
+            nc.vector.scalar_tensor_tensor(
+                out=result[:].rearrange("n g m -> n (g m)"),
+                in0=abs_cov[:].rearrange("n g m -> n (g m)"),
+                scalar=beta_f32[:],
+                in1=inv_denom[:].rearrange("n g m -> n (g m)"),
+                op0=ALU.mult,
+                op1=ALU.mult,
+            )
+            graphs = out[PAIR * pair : PAIR * (pair + 1)]
+            nc.sync.dma_start(out=graphs.rearrange("b n m -> n b m"), in_=result[:])
+
+        def run(stage, pair):
+            if 0 <= pair < PAIRS:
+                stage(pair)
+
+        for i in range(PAIRS + 4):
+            run(transpose_h, i)
+            run(transpose_x, i - 3)
+            run(spread_norm, i - 4)
+            run(project, i - 1)
+            run(correlate, i - 4)
+            run(centre, i - 2)
+            run(quantise_h, i)
+            run(take_moments, i - 1)
+            run(quantise_x, i - 3)
+            run(normalise, i - 4)

@@ -76,9 +76,11 @@ def tile_pearsonattention_pa_t_kernel(tc, h, W_h_words, W_h_scales, beta, out):
         nc.sync.dma_start(out=beta_bf16[:], in_=beta.partition_broadcast(P))
         for pair in range(1, PAIRS):
             load_h(pair)
-        nc.vector.tensor_copy(out=beta_f32[:], in_=beta_bf16[:])
+        nc.gpsimd.tensor_copy(out=beta_f32[:], in_=beta_bf16[:])
 
-        h_t, h_q, wh, neg_means, norms, x_m, x_t, x_q, epi = {}, {}, {}, {}, {}, {}, {}, {}, {}
+        h_t, h_g, h_q, wh, moments, norms, x_m, x_t, x_g, x_q, epi, factors = (
+            {}, {}, {}, {}, {}, {}, {}, {}, {}, {}, {}, {},
+        )
 
         def regroup(engine_copy, transposed, kind):
             grouped = work.tile([P, PAIR * NODES * 2 * HALVES], BF16, align_bytes=64, name=kind + "_grouped")
@@ -102,8 +104,11 @@ def tile_pearsonattention_pa_t_kernel(tc, h, W_h_words, W_h_scales, beta, out):
                     nc.tensor.transpose(transposed[:, g, u, :], words[:, u : F_IN // 2 : HALVES], ident[:])
             h_t[pair] = transposed
 
+        def regroup_h(pair):
+            h_g[pair] = regroup(nc.scalar.copy, h_t[pair], "h")
+
         def quantise_h(pair):
-            h_q[pair] = quantise(regroup(nc.scalar.copy, h_t[pair], "h"), "h")
+            h_q[pair] = quantise(h_g[pair], "h")
 
         def project(pair):
             codes, scales = h_q[pair]
@@ -127,33 +132,30 @@ def tile_pearsonattention_pa_t_kernel(tc, h, W_h_words, W_h_scales, beta, out):
                 partial = stat.tile([P, 6], F32, name="partial")
                 nc.vector.bn_stats(out=partial[:], in_=wh[(pair, g)][:])
                 nc.vector.bn_aggr(out=mean_var[:, g, :], in_=partial[:])
-            neg_mean = stat.tile([P, PAIR], F32, name="neg_mean")
-            nc.vector.tensor_scalar_mul(out=neg_mean[:], in0=mean_var[:, :, 0], scalar1=-1.0)
-            inv_norm = stat.tile([P, PAIR], F32, name="inv_norm")
+            moments[pair] = mean_var
+
+        def take_norm(pair):
+            variance = moments[pair][:, :, 1]
+            inv_root = stat.tile([P, PAIR], F32, name="inv_root")
             nc.scalar.activation(
-                out=inv_norm[:], in_=mean_var[:, :, 1], func=ACT.Abs_reciprocal_sqrt,
-                bias=tiny[:], scale=float(F_OUT),
+                out=inv_root[:], in_=variance, func=ACT.Abs_reciprocal_sqrt,
+                bias=tiny[:], scale=1.0 / F_OUT,
             )
             norm = stat.tile([P, PAIR], F32, name="norm")
-            nc.vector.scalar_tensor_tensor(
-                out=norm[:], in0=mean_var[:, :, 1], scalar=float(F_OUT), in1=inv_norm[:],
-                op0=ALU.mult, op1=ALU.mult,
-            )
-            neg_means[pair] = neg_mean
+            nc.gpsimd.tensor_tensor(out=norm[:], in0=variance, in1=inv_root[:], op=ALU.mult)
             norms[pair] = norm
 
         def centre(pair):
-            neg_mean = neg_means[pair]
-            centred = work.tile([P, PAIR, F_OUT], BF16, name="centred")
+            neg_centred = work.tile([P, PAIR, F_OUT], BF16, name="neg_centred")
             for g in range(PAIR):
                 nc.scalar.activation(
-                    out=centred[:, g, :].rearrange("n (u p e) -> n u p e", u=HALVES, e=2),
+                    out=neg_centred[:, g, :].rearrange("n (u p e) -> n u p e", u=HALVES, e=2),
                     in_=wh[(pair, g)][:].rearrange("n (p u e) -> n u p e", u=HALVES, e=2),
                     func=ACT.Identity,
-                    bias=neg_mean[:, g : g + 1],
-                    scale=1.0,
+                    bias=moments[pair][:, g, 0:1],
+                    scale=-1.0,
                 )
-            x_m[pair] = centred
+            x_m[pair] = neg_centred
 
         def transpose_x(pair):
             transposed = psum_xt.tile([P, PAIR, HALVES, NODES], F32, name="x_transposed")
@@ -163,14 +165,16 @@ def tile_pearsonattention_pa_t_kernel(tc, h, W_h_words, W_h_scales, beta, out):
                     nc.tensor.transpose(transposed[:, g, u, :], words[:, P * u : P * (u + 1)], ident[:])
             x_t[pair] = transposed
 
+        def regroup_x(pair):
+            x_g[pair] = regroup(nc.vector.tensor_copy, x_t[pair], "x")
+
         def quantise_x(pair):
-            x_q[pair] = quantise(regroup(nc.vector.tensor_copy, x_t[pair], "x"), "x")
+            x_q[pair] = quantise(x_g[pair], "x")
 
         def spread_norm(pair):
-            norm = norms[pair]
             bank = psum_epi.tile([P, 2, PAIR, NODES], F32, name="epi_bank")
             for g in range(PAIR):
-                nc.tensor.transpose(bank[:, 0, g, :], norm[:, g : g + 1].to_broadcast([P, P]), ident[:])
+                nc.tensor.transpose(bank[:, 0, g, :], norms[pair][:, g : g + 1].to_broadcast([P, P]), ident[:])
             epi[pair] = bank
 
         def correlate(pair):
@@ -187,19 +191,22 @@ def tile_pearsonattention_pa_t_kernel(tc, h, W_h_words, W_h_scales, beta, out):
                     stop=True,
                 )
 
-        def normalise(pair):
-            norm = norms[pair]
+        def take_factors(pair):
             bank = epi[pair]
             root = work.tile([P, PAIR, NODES], F32, name="root")
             for g in range(PAIR):
                 nc.scalar.activation(
                     out=root[:, g, :], in_=bank[:, 0, g, :], func=ACT.Abs_reciprocal_sqrt,
-                    bias=eps[:], scale=norm[:, g : g + 1],
+                    bias=eps[:], scale=norms[pair][:, g : g + 1],
                 )
             inv_denom = work.tile([P, PAIR, NODES], F32, name="inv_denom")
             nc.scalar.square(out=inv_denom[:], in_=root[:])
             abs_cov = work.tile([P, PAIR, NODES], F32, name="abs_cov")
             nc.scalar.activation(out=abs_cov[:], in_=bank[:, 1, :, :], func=ACT.Abs)
+            factors[pair] = (abs_cov, inv_denom)
+
+        def finish(pair):
+            abs_cov, inv_denom = factors[pair]
             result = res_pool.tile([P, PAIR, NODES], F32, name="result")
             nc.vector.scalar_tensor_tensor(
                 out=result[:].rearrange("n g m -> n (g m)"),
@@ -216,14 +223,19 @@ def tile_pearsonattention_pa_t_kernel(tc, h, W_h_words, W_h_scales, beta, out):
             if 0 <= pair < PAIRS:
                 stage(pair)
 
-        for i in range(PAIRS + 4):
-            run(transpose_h, i)
-            run(transpose_x, i - 3)
-            run(spread_norm, i - 4)
-            run(project, i - 1)
-            run(correlate, i - 4)
-            run(centre, i - 2)
-            run(quantise_h, i)
-            run(take_moments, i - 1)
-            run(quantise_x, i - 3)
-            run(normalise, i - 4)
+        with tc.manual_schedule():
+            for i in range(PAIRS + 4):
+                run(transpose_h, i)
+                run(transpose_x, i - 2)
+                run(spread_norm, i - 3)
+                run(correlate, i - 3)
+                run(take_factors, i - 4)
+                run(take_moments, i - 1)
+                run(regroup_h, i)
+                run(centre, i - 1)
+                run(regroup_x, i - 2)
+                run(quantise_h, i)
+                run(project, i)
+                run(finish, i - 4)
+                run(take_norm, i - 1)
+                run(quantise_x, i - 2)

@@ -78,8 +78,8 @@ def tile_pearsonattention_pa_t_kernel(tc, h, W_h_words, W_h_scales, beta, out):
             load_h(pair)
         nc.gpsimd.tensor_copy(out=beta_f32[:], in_=beta_bf16[:])
 
-        h_t, h_g, h_q, wh, moments, norms, x_m, x_t, x_g, x_q, epi, factors = (
-            {}, {}, {}, {}, {}, {}, {}, {}, {}, {}, {}, {},
+        h_t, h_g, h_q, wh, moments, norms, x_m, x_t, x_g, x_q, epi, roots, factors = (
+            {}, {}, {}, {}, {}, {}, {}, {}, {}, {}, {}, {}, {},
         )
 
         def regroup(engine_copy, transposed, kind):
@@ -191,18 +191,20 @@ def tile_pearsonattention_pa_t_kernel(tc, h, W_h_words, W_h_scales, beta, out):
                     stop=True,
                 )
 
-        def take_factors(pair):
-            bank = epi[pair]
+        def take_root(pair):
             root = work.tile([P, PAIR, NODES], F32, name="root")
             for g in range(PAIR):
                 nc.scalar.activation(
-                    out=root[:, g, :], in_=bank[:, 0, g, :], func=ACT.Abs_reciprocal_sqrt,
+                    out=root[:, g, :], in_=epi[pair][:, 0, g, :], func=ACT.Abs_reciprocal_sqrt,
                     bias=eps[:], scale=norms[pair][:, g : g + 1],
                 )
+            roots[pair] = root
+
+        def take_factors(pair):
             inv_denom = work.tile([P, PAIR, NODES], F32, name="inv_denom")
-            nc.scalar.square(out=inv_denom[:], in_=root[:])
+            nc.scalar.square(out=inv_denom[:], in_=roots[pair][:])
             abs_cov = work.tile([P, PAIR, NODES], F32, name="abs_cov")
-            nc.scalar.activation(out=abs_cov[:], in_=bank[:, 1, :, :], func=ACT.Abs)
+            nc.scalar.activation(out=abs_cov[:], in_=epi[pair][:, 1, :, :], func=ACT.Abs)
             factors[pair] = (abs_cov, inv_denom)
 
         def finish(pair):
@@ -224,18 +226,19 @@ def tile_pearsonattention_pa_t_kernel(tc, h, W_h_words, W_h_scales, beta, out):
                 stage(pair)
 
         with tc.manual_schedule():
-            for i in range(PAIRS + 4):
+            for i in range(PAIRS + 6):
                 run(transpose_h, i)
-                run(transpose_x, i - 2)
-                run(spread_norm, i - 3)
-                run(correlate, i - 3)
-                run(take_factors, i - 4)
-                run(take_moments, i - 1)
+                run(take_factors, i - 6)
+                run(centre, i - 3)
+                run(correlate, i - 5)
+                run(regroup_x, i - 4)
+                run(project, i - 2)
+                run(quantise_h, i - 1)
+                run(finish, i - 6)
                 run(regroup_h, i)
-                run(centre, i - 1)
-                run(regroup_x, i - 2)
-                run(quantise_h, i)
-                run(project, i)
-                run(finish, i - 4)
-                run(take_norm, i - 1)
-                run(quantise_x, i - 2)
+                run(quantise_x, i - 4)
+                run(take_moments, i - 2)
+                run(transpose_x, i - 3)
+                run(take_norm, i - 3)
+                run(take_root, i - 5)
+                run(spread_norm, i - 4)

@@ -21,6 +21,9 @@ HALVES = 2
 PAIR = 2
 PAIRS = GRAPHS // PAIR
 EPS = 1e-8
+WORK = 3
+STAT = 8
+RESULTS = 6
 TINY = 1e-36
 
 FLOPS = 2 * GRAPHS * NODES * F_IN * F_OUT + 2 * GRAPHS * NODES * NODES * F_OUT
@@ -31,13 +34,11 @@ def tile_pearsonattention_pa_t_kernel(tc, h, W_h_words, W_h_scales, beta, out):
     with ExitStack() as ctx:
         const = ctx.enter_context(tc.tile_pool(name="const", bufs=1))
         h_pool = ctx.enter_context(tc.tile_pool(name="h_pool", bufs=PAIRS))
-        work = ctx.enter_context(tc.tile_pool(name="work", bufs=3))
-        stat = ctx.enter_context(tc.tile_pool(name="stat", bufs=8))
-        res_pool = ctx.enter_context(tc.tile_pool(name="res_pool", bufs=6))
-        psum_ht = ctx.enter_context(tc.psum_pool(name="psum_ht", bufs=1))
-        psum_xt = ctx.enter_context(tc.psum_pool(name="psum_xt", bufs=1))
-        psum_wh = ctx.enter_context(tc.psum_pool(name="psum_wh", bufs=2 * PAIR))
-        psum_epi = ctx.enter_context(tc.psum_pool(name="psum_epi", bufs=2))
+        sbuf = ctx.enter_context(tc.tile_pool(name="sbuf", bufs=1))
+        psum = ctx.enter_context(tc.psum_pool(name="psum", bufs=1))
+
+        def ring(pool, depth, index, shape, dtype, name, **how):
+            return pool.tile(shape, dtype, name=name, tag="%s_%d" % (name, index % depth), **how)
 
         eps = const.tile([P, 1], F32)
         nc.vector.memset(eps[:], EPS)
@@ -78,26 +79,27 @@ def tile_pearsonattention_pa_t_kernel(tc, h, W_h_words, W_h_scales, beta, out):
             load_h(pair)
         nc.gpsimd.tensor_copy(out=beta_f32[:], in_=beta_bf16[:])
 
-        h_t, h_g, h_q, wh, moments, norms, x_m, x_t, x_g, x_q, epi, roots, factors = (
+        h_t, h_g, h_q, wh, partials, moments, norms, x_m, x_t, x_g, x_q, epi, roots = (
             {}, {}, {}, {}, {}, {}, {}, {}, {}, {}, {}, {}, {},
         )
+        abs_covs, inv_denoms = {}, {}
 
-        def regroup(engine_copy, transposed, kind):
-            grouped = work.tile([P, PAIR * NODES * 2 * HALVES], BF16, align_bytes=64, name=kind + "_grouped")
+        def regroup(engine_copy, transposed, kind, pair):
+            grouped = ring(sbuf, WORK, pair, [P, PAIR * NODES * 2 * HALVES], BF16, kind + "_grouped", align_bytes=64)
             engine_copy(
                 out=grouped[:].bitcast(F32).rearrange("p (g n u) -> p g n u", g=PAIR, u=HALVES),
                 in_=transposed[:].rearrange("p g u n -> p g n u"),
             )
             return grouped
 
-        def quantise(grouped, kind):
-            codes = work.tile([P, PAIR * NODES], U32, align_bytes=64, name=kind + "_codes")
-            scales = work.tile([P, PAIR * NODES], U8, align_bytes=64, name=kind + "_scales")
+        def quantise(grouped, kind, pair):
+            codes = ring(sbuf, WORK, pair, [P, PAIR * NODES], U32, kind + "_codes", align_bytes=64)
+            scales = ring(sbuf, WORK, pair, [P, PAIR * NODES], U8, kind + "_scales", align_bytes=64)
             nc.vector.quantize_mx(out=codes[:].bitcast(FP8X4), scales=scales[:], in_=grouped[:])
             return codes, scales
 
         def transpose_h(pair):
-            transposed = psum_ht.tile([P, PAIR, HALVES, NODES], F32, name="h_transposed")
+            transposed = ring(psum, 1, pair, [P, PAIR, HALVES, NODES], F32, "h_transposed")
             for g in range(PAIR):
                 words = h_pairs[pair][:, g, :].bitcast(F32)
                 for u in range(HALVES):
@@ -105,16 +107,16 @@ def tile_pearsonattention_pa_t_kernel(tc, h, W_h_words, W_h_scales, beta, out):
             h_t[pair] = transposed
 
         def regroup_h(pair):
-            h_g[pair] = regroup(nc.scalar.copy, h_t[pair], "h")
+            h_g[pair] = regroup(nc.scalar.copy, h_t[pair], "h", pair)
 
         def quantise_h(pair):
-            h_q[pair] = quantise(h_g[pair], "h")
+            h_q[pair] = quantise(h_g[pair], "h", pair)
 
         def project(pair):
             codes, scales = h_q[pair]
             for g in range(PAIR):
                 nodes = slice(NODES * g, NODES * (g + 1))
-                acc = psum_wh.tile([P, F_OUT], F32, name="wh_acc")
+                acc = ring(psum, 2 * PAIR, PAIR * pair + g, [P, F_OUT], F32, "wh_acc")
                 nc.tensor.matmul_mx(
                     out=acc[:],
                     lhsT=codes[:, nodes].bitcast(FP8X4),
@@ -126,27 +128,31 @@ def tile_pearsonattention_pa_t_kernel(tc, h, W_h_words, W_h_scales, beta, out):
                 )
                 wh[(pair, g)] = acc
 
-        def take_moments(pair):
-            mean_var = stat.tile([P, PAIR, 2], F32, name="mean_var")
+        def take_stats(pair):
             for g in range(PAIR):
-                partial = stat.tile([P, 6], F32, name="partial")
+                partial = ring(sbuf, STAT, PAIR * pair + g, [P, 6], F32, "partial")
                 nc.vector.bn_stats(out=partial[:], in_=wh[(pair, g)][:])
-                nc.vector.bn_aggr(out=mean_var[:, g, :], in_=partial[:])
+                partials[(pair, g)] = partial
+
+        def take_moments(pair):
+            mean_var = ring(sbuf, STAT, pair, [P, PAIR, 2], F32, "mean_var")
+            for g in range(PAIR):
+                nc.vector.bn_aggr(out=mean_var[:, g, :], in_=partials[(pair, g)][:])
             moments[pair] = mean_var
 
         def take_norm(pair):
             variance = moments[pair][:, :, 1]
-            inv_root = stat.tile([P, PAIR], F32, name="inv_root")
+            inv_root = ring(sbuf, STAT, pair, [P, PAIR], F32, "inv_root")
             nc.scalar.activation(
                 out=inv_root[:], in_=variance, func=ACT.Abs_reciprocal_sqrt,
                 bias=tiny[:], scale=1.0 / F_OUT,
             )
-            norm = stat.tile([P, PAIR], F32, name="norm")
+            norm = ring(sbuf, STAT, pair, [P, PAIR], F32, "norm")
             nc.gpsimd.tensor_tensor(out=norm[:], in0=variance, in1=inv_root[:], op=ALU.mult)
             norms[pair] = norm
 
         def centre(pair):
-            neg_centred = work.tile([P, PAIR, F_OUT], BF16, name="neg_centred")
+            neg_centred = ring(sbuf, WORK, pair, [P, PAIR, F_OUT], BF16, "neg_centred")
             for g in range(PAIR):
                 nc.scalar.activation(
                     out=neg_centred[:, g, :].rearrange("n (u p e) -> n u p e", u=HALVES, e=2),
@@ -158,7 +164,7 @@ def tile_pearsonattention_pa_t_kernel(tc, h, W_h_words, W_h_scales, beta, out):
             x_m[pair] = neg_centred
 
         def transpose_x(pair):
-            transposed = psum_xt.tile([P, PAIR, HALVES, NODES], F32, name="x_transposed")
+            transposed = ring(psum, 1, pair, [P, PAIR, HALVES, NODES], F32, "x_transposed")
             for g in range(PAIR):
                 words = x_m[pair][:, g, :].bitcast(F32)
                 for u in range(HALVES):
@@ -166,13 +172,13 @@ def tile_pearsonattention_pa_t_kernel(tc, h, W_h_words, W_h_scales, beta, out):
             x_t[pair] = transposed
 
         def regroup_x(pair):
-            x_g[pair] = regroup(nc.vector.tensor_copy, x_t[pair], "x")
+            x_g[pair] = regroup(nc.vector.tensor_copy, x_t[pair], "x", pair)
 
         def quantise_x(pair):
-            x_q[pair] = quantise(x_g[pair], "x")
+            x_q[pair] = quantise(x_g[pair], "x", pair)
 
         def spread_norm(pair):
-            bank = psum_epi.tile([P, 2, PAIR, NODES], F32, name="epi_bank")
+            bank = ring(psum, 2, pair, [P, 2, PAIR, NODES], F32, "epi_bank")
             for g in range(PAIR):
                 nc.tensor.transpose(bank[:, 0, g, :], norms[pair][:, g : g + 1].to_broadcast([P, P]), ident[:])
             epi[pair] = bank
@@ -192,7 +198,7 @@ def tile_pearsonattention_pa_t_kernel(tc, h, W_h_words, W_h_scales, beta, out):
                 )
 
         def take_root(pair):
-            root = work.tile([P, PAIR, NODES], F32, name="root")
+            root = ring(sbuf, WORK, pair, [P, PAIR, NODES], F32, "root")
             for g in range(PAIR):
                 nc.scalar.activation(
                     out=root[:, g, :], in_=epi[pair][:, 0, g, :], func=ACT.Abs_reciprocal_sqrt,
@@ -200,16 +206,19 @@ def tile_pearsonattention_pa_t_kernel(tc, h, W_h_words, W_h_scales, beta, out):
                 )
             roots[pair] = root
 
-        def take_factors(pair):
-            inv_denom = work.tile([P, PAIR, NODES], F32, name="inv_denom")
+        def square_root(pair):
+            inv_denom = ring(sbuf, WORK, pair, [P, PAIR, NODES], F32, "inv_denom")
             nc.scalar.square(out=inv_denom[:], in_=roots[pair][:])
-            abs_cov = work.tile([P, PAIR, NODES], F32, name="abs_cov")
+            inv_denoms[pair] = inv_denom
+
+        def take_abs(pair):
+            abs_cov = ring(sbuf, WORK, pair, [P, PAIR, NODES], F32, "abs_cov")
             nc.scalar.activation(out=abs_cov[:], in_=epi[pair][:, 1, :, :], func=ACT.Abs)
-            factors[pair] = (abs_cov, inv_denom)
+            abs_covs[pair] = abs_cov
 
         def finish(pair):
-            abs_cov, inv_denom = factors[pair]
-            result = res_pool.tile([P, PAIR, NODES], F32, name="result")
+            abs_cov, inv_denom = abs_covs[pair], inv_denoms[pair]
+            result = ring(sbuf, RESULTS, pair, [P, PAIR, NODES], F32, "result")
             nc.vector.scalar_tensor_tensor(
                 out=result[:].rearrange("n g m -> n (g m)"),
                 in0=abs_cov[:].rearrange("n g m -> n (g m)"),
@@ -226,19 +235,21 @@ def tile_pearsonattention_pa_t_kernel(tc, h, W_h_words, W_h_scales, beta, out):
                 stage(pair)
 
         with tc.manual_schedule():
-            for i in range(PAIRS + 6):
+            for i in range(PAIRS + 7):
+                run(quantise_x, i - 5)
                 run(transpose_h, i)
-                run(take_factors, i - 6)
-                run(centre, i - 3)
-                run(correlate, i - 5)
-                run(regroup_x, i - 4)
-                run(project, i - 2)
-                run(quantise_h, i - 1)
-                run(finish, i - 6)
-                run(regroup_h, i)
-                run(quantise_x, i - 4)
-                run(take_moments, i - 2)
-                run(transpose_x, i - 3)
-                run(take_norm, i - 3)
-                run(take_root, i - 5)
+                run(transpose_x, i - 4)
                 run(spread_norm, i - 4)
+                run(correlate, i - 5)
+                run(project, i - 1)
+                run(take_stats, i - 2)
+                run(regroup_x, i - 4)
+                run(take_moments, i - 2)
+                run(finish, i - 7)
+                run(take_abs, i - 6)
+                run(centre, i - 3)
+                run(regroup_h, i)
+                run(take_norm, i - 3)
+                run(square_root, i - 6)
+                run(take_root, i - 5)
+                run(quantise_h, i)

@@ -79,10 +79,8 @@ def tile_pearsonattention_pa_t_kernel(tc, h, W_h_words, W_h_scales, beta, out):
             load_h(pair)
         nc.gpsimd.tensor_copy(out=beta_f32[:], in_=beta_bf16[:])
 
-        h_t, h_g, h_q, wh, partials, moments, norms, x_m, x_t, x_g, x_q, epi, roots = (
-            {}, {}, {}, {}, {}, {}, {}, {}, {}, {}, {}, {}, {},
-        )
-        abs_covs, inv_denoms = {}, {}
+        h_t, h_g, h_q, wh, partials, moments, norms, x_m, x_t, x_g, x_q = {}, {}, {}, {}, {}, {}, {}, {}, {}, {}, {}
+        spread, covs, roots, abs_covs, inv_denoms = {}, {}, {}, {}, {}
 
         def regroup(engine_copy, transposed, kind, pair):
             grouped = ring(sbuf, WORK, pair, [P, PAIR * NODES * 2 * HALVES], BF16, kind + "_grouped", align_bytes=64)
@@ -172,23 +170,27 @@ def tile_pearsonattention_pa_t_kernel(tc, h, W_h_words, W_h_scales, beta, out):
             x_t[pair] = transposed
 
         def regroup_x(pair):
-            x_g[pair] = regroup(nc.vector.tensor_copy, x_t[pair], "x", pair)
+            engine_copy = nc.scalar.copy if pair % 2 else nc.vector.tensor_copy
+            x_g[pair] = regroup(engine_copy, x_t[pair], "x", pair)
 
         def quantise_x(pair):
             x_q[pair] = quantise(x_g[pair], "x", pair)
 
         def spread_norm(pair):
-            bank = ring(psum, 2, pair, [P, 2, PAIR, NODES], F32, "epi_bank")
+            bank = ring(psum, 1, pair, [P, PAIR, NODES], F32, "spread")
             for g in range(PAIR):
-                nc.tensor.transpose(bank[:, 0, g, :], norms[pair][:, g : g + 1].to_broadcast([P, P]), ident[:])
-            epi[pair] = bank
+                nc.tensor.transpose(bank[:, g, :], norms[pair][:, g : g + 1].to_broadcast([P, P]), ident[:])
+            spread[pair] = bank
 
         def correlate(pair):
+            quad, half = divmod(pair, 2)
+            if half == 0:
+                covs[quad] = ring(psum, 1, quad, [P, 2 * PAIR, NODES], F32, "cov")
             codes, scales = x_q[pair]
             for g in range(PAIR):
                 nodes = slice(NODES * g, NODES * (g + 1))
                 nc.tensor.matmul_mx(
-                    out=epi[pair][:, 1, g, :],
+                    out=covs[quad][:, PAIR * half + g, :],
                     lhsT=codes[:, nodes].bitcast(FP8X4),
                     lhsT_scale=scales[:, nodes],
                     rhs=codes[:, nodes].bitcast(FP8X4),
@@ -201,55 +203,62 @@ def tile_pearsonattention_pa_t_kernel(tc, h, W_h_words, W_h_scales, beta, out):
             root = ring(sbuf, WORK, pair, [P, PAIR, NODES], F32, "root")
             for g in range(PAIR):
                 nc.scalar.activation(
-                    out=root[:, g, :], in_=epi[pair][:, 0, g, :], func=ACT.Abs_reciprocal_sqrt,
+                    out=root[:, g, :], in_=spread[pair][:, g, :], func=ACT.Abs_reciprocal_sqrt,
                     bias=eps[:], scale=norms[pair][:, g : g + 1],
                 )
             roots[pair] = root
 
         def square_root(pair):
-            inv_denom = ring(sbuf, WORK, pair, [P, PAIR, NODES], F32, "inv_denom")
-            nc.scalar.square(out=inv_denom[:], in_=roots[pair][:])
-            inv_denoms[pair] = inv_denom
+            quad, half = divmod(pair, 2)
+            if half == 0:
+                inv_denoms[quad] = ring(sbuf, WORK, quad, [P, 2 * PAIR, NODES], F32, "inv_denom")
+            root = roots[pair][:]
+            nc.gpsimd.tensor_tensor(
+                out=inv_denoms[quad][:, PAIR * half : PAIR * (half + 1), :], in0=root, in1=root, op=ALU.mult,
+            )
 
-        def take_abs(pair):
-            abs_cov = ring(sbuf, WORK, pair, [P, PAIR, NODES], F32, "abs_cov")
-            nc.scalar.activation(out=abs_cov[:], in_=epi[pair][:, 1, :, :], func=ACT.Abs)
-            abs_covs[pair] = abs_cov
+        def take_abs(quad):
+            abs_cov = ring(sbuf, WORK, quad, [P, 2 * PAIR, NODES], F32, "abs_cov")
+            nc.scalar.activation(out=abs_cov[:], in_=covs[quad][:], func=ACT.Abs)
+            abs_covs[quad] = abs_cov
 
-        def finish(pair):
-            abs_cov, inv_denom = abs_covs[pair], inv_denoms[pair]
-            result = ring(sbuf, RESULTS, pair, [P, PAIR, NODES], F32, "result")
+        def finish(quad):
+            result = ring(sbuf, RESULTS, quad, [P, 2 * PAIR, NODES], F32, "result")
             nc.vector.scalar_tensor_tensor(
                 out=result[:].rearrange("n g m -> n (g m)"),
-                in0=abs_cov[:].rearrange("n g m -> n (g m)"),
+                in0=abs_covs[quad][:].rearrange("n g m -> n (g m)"),
                 scalar=beta_f32[:],
-                in1=inv_denom[:].rearrange("n g m -> n (g m)"),
+                in1=inv_denoms[quad][:].rearrange("n g m -> n (g m)"),
                 op0=ALU.mult,
                 op1=ALU.mult,
             )
-            graphs = out[PAIR * pair : PAIR * (pair + 1)]
+            graphs = out[2 * PAIR * quad : 2 * PAIR * (quad + 1)]
             nc.sync.dma_start(out=graphs.rearrange("b n m -> n b m"), in_=result[:])
 
         def run(stage, pair):
             if 0 <= pair < PAIRS:
                 stage(pair)
 
+        def run_quad(stage, pair):
+            if 0 <= pair < PAIRS and pair % 2 == 1:
+                stage(pair // 2)
+
         with tc.manual_schedule():
             for i in range(PAIRS + 7):
                 run(quantise_x, i - 5)
-                run(transpose_h, i)
                 run(transpose_x, i - 4)
-                run(spread_norm, i - 4)
+                run(transpose_h, i)
+                run(take_root, i - 6)
+                run(square_root, i - 6)
+                run(spread_norm, i - 5)
                 run(correlate, i - 5)
-                run(project, i - 1)
                 run(take_stats, i - 2)
-                run(regroup_x, i - 4)
-                run(take_moments, i - 2)
-                run(finish, i - 7)
-                run(take_abs, i - 6)
                 run(centre, i - 3)
                 run(regroup_h, i)
+                run(project, i - 1)
+                run(regroup_x, i - 4)
+                run_quad(finish, i - 6)
+                run(take_moments, i - 2)
+                run_quad(take_abs, i - 5)
                 run(take_norm, i - 3)
-                run(square_root, i - 6)
-                run(take_root, i - 5)
                 run(quantise_h, i)

@@ -24,6 +24,7 @@ EPS = 1e-8
 WORK = 3
 STAT = 8
 RESULTS = 6
+SHARE = 96
 TINY = 1e-36
 
 FLOPS = 2 * GRAPHS * NODES * F_IN * F_OUT + 2 * GRAPHS * NODES * NODES * F_OUT
@@ -80,15 +81,16 @@ def tile_pearsonattention_pa_t_kernel(tc, h, W_h_words, W_h_scales, beta, out):
         nc.gpsimd.tensor_copy(out=beta_f32[:], in_=beta_bf16[:])
 
         h_t, h_g, h_q, wh, partials, moments, norms, x_m, x_t, x_g, x_q = {}, {}, {}, {}, {}, {}, {}, {}, {}, {}, {}
-        spread, covs, roots, abs_covs, inv_denoms = {}, {}, {}, {}, {}
+        inv_roots, spread, covs, roots, abs_covs, inv_denoms = {}, {}, {}, {}, {}, {}
 
-        def regroup(engine_copy, transposed, kind, pair):
-            grouped = ring(sbuf, WORK, pair, [P, PAIR * NODES * 2 * HALVES], BF16, kind + "_grouped", align_bytes=64)
+        def new_grouped(kind, pair):
+            return ring(sbuf, WORK, pair, [P, PAIR * NODES * 2 * HALVES], BF16, kind + "_grouped", align_bytes=64)
+
+        def regroup(engine_copy, transposed, grouped, nodes):
             engine_copy(
-                out=grouped[:].bitcast(F32).rearrange("p (g n u) -> p g n u", g=PAIR, u=HALVES),
-                in_=transposed[:].rearrange("p g u n -> p g n u"),
+                out=grouped[:].bitcast(F32).rearrange("p (g n u) -> p g n u", g=PAIR, u=HALVES)[:, :, nodes, :],
+                in_=transposed[:].rearrange("p g u n -> p g n u")[:, :, nodes, :],
             )
-            return grouped
 
         def quantise(grouped, kind, pair):
             codes = ring(sbuf, WORK, pair, [P, PAIR * NODES], U32, kind + "_codes", align_bytes=64)
@@ -105,7 +107,8 @@ def tile_pearsonattention_pa_t_kernel(tc, h, W_h_words, W_h_scales, beta, out):
             h_t[pair] = transposed
 
         def regroup_h(pair):
-            h_g[pair] = regroup(nc.scalar.copy, h_t[pair], "h", pair)
+            h_g[pair] = new_grouped("h", pair)
+            regroup(nc.scalar.copy, h_t[pair], h_g[pair], slice(0, NODES))
 
         def quantise_h(pair):
             h_q[pair] = quantise(h_g[pair], "h", pair)
@@ -133,21 +136,25 @@ def tile_pearsonattention_pa_t_kernel(tc, h, W_h_words, W_h_scales, beta, out):
                 partials[(pair, g)] = partial
 
         def take_moments(pair):
-            mean_var = ring(sbuf, STAT, pair, [P, PAIR, 2], F32, "mean_var")
+            quad, half = divmod(pair, 2)
+            if half == 0:
+                moments[quad] = ring(sbuf, STAT, quad, [P, 2 * PAIR, 2], F32, "mean_var")
             for g in range(PAIR):
-                nc.vector.bn_aggr(out=mean_var[:, g, :], in_=partials[(pair, g)][:])
-            moments[pair] = mean_var
+                nc.vector.bn_aggr(out=moments[quad][:, PAIR * half + g, :], in_=partials[(pair, g)][:])
 
-        def take_norm(pair):
-            variance = moments[pair][:, :, 1]
-            inv_root = ring(sbuf, STAT, pair, [P, PAIR], F32, "inv_root")
+        def invert_root(quad):
+            inv_root = ring(sbuf, STAT, quad, [P, 2 * PAIR], F32, "inv_root")
             nc.scalar.activation(
-                out=inv_root[:], in_=variance, func=ACT.Abs_reciprocal_sqrt,
+                out=inv_root[:], in_=moments[quad][:, :, 1], func=ACT.Abs_reciprocal_sqrt,
                 bias=tiny[:], scale=1.0 / F_OUT,
             )
-            norm = ring(sbuf, STAT, pair, [P, PAIR], F32, "norm")
-            nc.gpsimd.tensor_tensor(out=norm[:], in0=variance, in1=inv_root[:], op=ALU.mult)
-            norms[pair] = norm
+            inv_roots[quad] = inv_root
+
+        def take_norm(quad):
+            norm = ring(sbuf, STAT, quad, [P, 2 * PAIR], F32, "norm")
+            nc.gpsimd.tensor_tensor(out=norm[:], in0=moments[quad][:, :, 1], in1=inv_roots[quad][:], op=ALU.mult)
+            for g in range(2 * PAIR):
+                norms[2 * PAIR * quad + g] = norm[:, g : g + 1]
 
         def centre(pair):
             neg_centred = ring(sbuf, WORK, pair, [P, PAIR, F_OUT], BF16, "neg_centred")
@@ -156,7 +163,7 @@ def tile_pearsonattention_pa_t_kernel(tc, h, W_h_words, W_h_scales, beta, out):
                     out=neg_centred[:, g, :].rearrange("n (u p e) -> n u p e", u=HALVES, e=2),
                     in_=wh[(pair, g)][:].rearrange("n (p u e) -> n u p e", u=HALVES, e=2),
                     func=ACT.Identity,
-                    bias=moments[pair][:, g, 0:1],
+                    bias=moments[pair // 2][:, PAIR * (pair % 2) + g, 0:1],
                     scale=-1.0,
                 )
             x_m[pair] = neg_centred
@@ -169,9 +176,12 @@ def tile_pearsonattention_pa_t_kernel(tc, h, W_h_words, W_h_scales, beta, out):
                     nc.tensor.transpose(transposed[:, g, u, :], words[:, P * u : P * (u + 1)], ident[:])
             x_t[pair] = transposed
 
-        def regroup_x(pair):
-            engine_copy = nc.scalar.copy if pair % 2 else nc.vector.tensor_copy
-            x_g[pair] = regroup(engine_copy, x_t[pair], "x", pair)
+        def regroup_x_scalar(pair):
+            x_g[pair] = new_grouped("x", pair)
+            regroup(nc.scalar.copy, x_t[pair], x_g[pair], slice(SHARE, NODES))
+
+        def regroup_x_vector(pair):
+            regroup(nc.vector.tensor_copy, x_t[pair], x_g[pair], slice(0, SHARE))
 
         def quantise_x(pair):
             x_q[pair] = quantise(x_g[pair], "x", pair)
@@ -179,18 +189,16 @@ def tile_pearsonattention_pa_t_kernel(tc, h, W_h_words, W_h_scales, beta, out):
         def spread_norm(pair):
             bank = ring(psum, 1, pair, [P, PAIR, NODES], F32, "spread")
             for g in range(PAIR):
-                nc.tensor.transpose(bank[:, g, :], norms[pair][:, g : g + 1].to_broadcast([P, P]), ident[:])
+                nc.tensor.transpose(bank[:, g, :], norms[PAIR * pair + g].to_broadcast([P, P]), ident[:])
             spread[pair] = bank
 
         def correlate(pair):
-            quad, half = divmod(pair, 2)
-            if half == 0:
-                covs[quad] = ring(psum, 1, quad, [P, 2 * PAIR, NODES], F32, "cov")
+            bank = ring(psum, 1, pair, [P, PAIR, NODES], F32, "cov")
             codes, scales = x_q[pair]
             for g in range(PAIR):
                 nodes = slice(NODES * g, NODES * (g + 1))
                 nc.tensor.matmul_mx(
-                    out=covs[quad][:, PAIR * half + g, :],
+                    out=bank[:, g, :],
                     lhsT=codes[:, nodes].bitcast(FP8X4),
                     lhsT_scale=scales[:, nodes],
                     rhs=codes[:, nodes].bitcast(FP8X4),
@@ -198,41 +206,38 @@ def tile_pearsonattention_pa_t_kernel(tc, h, W_h_words, W_h_scales, beta, out):
                     start=True,
                     stop=True,
                 )
+            covs[pair] = bank
 
         def take_root(pair):
             root = ring(sbuf, WORK, pair, [P, PAIR, NODES], F32, "root")
             for g in range(PAIR):
                 nc.scalar.activation(
                     out=root[:, g, :], in_=spread[pair][:, g, :], func=ACT.Abs_reciprocal_sqrt,
-                    bias=eps[:], scale=norms[pair][:, g : g + 1],
+                    bias=eps[:], scale=norms[PAIR * pair + g],
                 )
             roots[pair] = root
 
         def square_root(pair):
-            quad, half = divmod(pair, 2)
-            if half == 0:
-                inv_denoms[quad] = ring(sbuf, WORK, quad, [P, 2 * PAIR, NODES], F32, "inv_denom")
-            root = roots[pair][:]
-            nc.gpsimd.tensor_tensor(
-                out=inv_denoms[quad][:, PAIR * half : PAIR * (half + 1), :], in0=root, in1=root, op=ALU.mult,
-            )
+            inv_denom = ring(sbuf, WORK, pair + 1, [P, PAIR, NODES], F32, "x_grouped", align_bytes=64)
+            nc.gpsimd.tensor_tensor(out=inv_denom[:], in0=roots[pair][:], in1=roots[pair][:], op=ALU.mult)
+            inv_denoms[pair] = inv_denom
 
-        def take_abs(quad):
-            abs_cov = ring(sbuf, WORK, quad, [P, 2 * PAIR, NODES], F32, "abs_cov")
-            nc.scalar.activation(out=abs_cov[:], in_=covs[quad][:], func=ACT.Abs)
-            abs_covs[quad] = abs_cov
+        def take_abs(pair):
+            abs_cov = ring(sbuf, WORK, pair, [P, PAIR, NODES], F32, "abs_cov")
+            nc.scalar.activation(out=abs_cov[:], in_=covs[pair][:], func=ACT.Abs)
+            abs_covs[pair] = abs_cov
 
-        def finish(quad):
-            result = ring(sbuf, RESULTS, quad, [P, 2 * PAIR, NODES], F32, "result")
+        def finish(pair):
+            result = ring(sbuf, RESULTS, pair, [P, PAIR, NODES], F32, "result")
             nc.vector.scalar_tensor_tensor(
                 out=result[:].rearrange("n g m -> n (g m)"),
-                in0=abs_covs[quad][:].rearrange("n g m -> n (g m)"),
+                in0=abs_covs[pair][:].rearrange("n g m -> n (g m)"),
                 scalar=beta_f32[:],
-                in1=inv_denoms[quad][:].rearrange("n g m -> n (g m)"),
+                in1=inv_denoms[pair][:].rearrange("n g m -> n (g m)"),
                 op0=ALU.mult,
                 op1=ALU.mult,
             )
-            graphs = out[2 * PAIR * quad : 2 * PAIR * (quad + 1)]
+            graphs = out[PAIR * pair : PAIR * (pair + 1)]
             nc.sync.dma_start(out=graphs.rearrange("b n m -> n b m"), in_=result[:])
 
         def run(stage, pair):
@@ -252,13 +257,15 @@ def tile_pearsonattention_pa_t_kernel(tc, h, W_h_words, W_h_scales, beta, out):
                 run(square_root, i - 6)
                 run(spread_norm, i - 5)
                 run(correlate, i - 5)
+                run(regroup_x_scalar, i - 4)
                 run(take_stats, i - 2)
                 run(centre, i - 3)
                 run(regroup_h, i)
                 run(project, i - 1)
-                run(regroup_x, i - 4)
-                run_quad(finish, i - 6)
+                run(regroup_x_vector, i - 4)
+                run(finish, i - 6)
                 run(take_moments, i - 2)
-                run_quad(take_abs, i - 5)
-                run(take_norm, i - 3)
+                run(take_abs, i - 5)
+                run_quad(invert_root, i - 3)
+                run_quad(take_norm, i - 3)
                 run(quantise_h, i)

@@ -24,7 +24,7 @@ EPS = 1e-8
 WORK = 3
 STAT = 8
 RESULTS = 6
-SHARE = 96
+SHARE = 80
 TINY = 1e-36
 
 FLOPS = 2 * GRAPHS * NODES * F_IN * F_OUT + 2 * GRAPHS * NODES * NODES * F_OUT
@@ -113,21 +113,26 @@ def tile_pearsonattention_pa_t_kernel(tc, h, W_h_words, W_h_scales, beta, out):
         def quantise_h(pair):
             h_q[pair] = quantise(h_g[pair], "h", pair)
 
-        def project(pair):
+        def project(pair, g):
             codes, scales = h_q[pair]
-            for g in range(PAIR):
-                nodes = slice(NODES * g, NODES * (g + 1))
-                acc = ring(psum, 2 * PAIR, PAIR * pair + g, [P, F_OUT], F32, "wh_acc")
-                nc.tensor.matmul_mx(
-                    out=acc[:],
-                    lhsT=codes[:, nodes].bitcast(FP8X4),
-                    lhsT_scale=scales[:, nodes],
-                    rhs=w_codes[:].bitcast(FP8X4),
-                    rhs_scale=w_scales[:],
-                    start=True,
-                    stop=True,
-                )
-                wh[(pair, g)] = acc
+            nodes = slice(NODES * g, NODES * (g + 1))
+            acc = ring(psum, 2 * PAIR, PAIR * pair + g, [P, F_OUT], F32, "wh_acc")
+            nc.tensor.matmul_mx(
+                out=acc[:],
+                lhsT=codes[:, nodes].bitcast(FP8X4),
+                lhsT_scale=scales[:, nodes],
+                rhs=w_codes[:].bitcast(FP8X4),
+                rhs_scale=w_scales[:],
+                start=True,
+                stop=True,
+            )
+            wh[(pair, g)] = acc
+
+        def project_first(pair):
+            project(pair, 0)
+
+        def project_second(pair):
+            project(pair, 1)
 
         def take_stats(pair):
             for g in range(PAIR):
@@ -176,12 +181,12 @@ def tile_pearsonattention_pa_t_kernel(tc, h, W_h_words, W_h_scales, beta, out):
                     nc.tensor.transpose(transposed[:, g, u, :], words[:, P * u : P * (u + 1)], ident[:])
             x_t[pair] = transposed
 
-        def regroup_x_scalar(pair):
-            x_g[pair] = new_grouped("x", pair)
-            regroup(nc.scalar.copy, x_t[pair], x_g[pair], slice(SHARE, NODES))
-
         def regroup_x_vector(pair):
+            x_g[pair] = new_grouped("x", pair)
             regroup(nc.vector.tensor_copy, x_t[pair], x_g[pair], slice(0, SHARE))
+
+        def regroup_x_scalar(pair):
+            regroup(nc.scalar.copy, x_t[pair], x_g[pair], slice(SHARE, NODES))
 
         def quantise_x(pair):
             x_q[pair] = quantise(x_g[pair], "x", pair)
@@ -218,7 +223,7 @@ def tile_pearsonattention_pa_t_kernel(tc, h, W_h_words, W_h_scales, beta, out):
             roots[pair] = root
 
         def square_root(pair):
-            inv_denom = ring(sbuf, WORK, pair + 1, [P, PAIR, NODES], F32, "x_grouped", align_bytes=64)
+            inv_denom = ring(sbuf, WORK, pair, [P, PAIR, NODES], F32, "x_grouped", align_bytes=64)
             nc.gpsimd.tensor_tensor(out=inv_denom[:], in0=roots[pair][:], in1=roots[pair][:], op=ALU.mult)
             inv_denoms[pair] = inv_denom
 
@@ -251,21 +256,22 @@ def tile_pearsonattention_pa_t_kernel(tc, h, W_h_words, W_h_scales, beta, out):
         with tc.manual_schedule():
             for i in range(PAIRS + 7):
                 run(quantise_x, i - 5)
+                run(quantise_h, i - 1)
+                run_quad(invert_root, i - 3)
+                run_quad(take_norm, i - 3)
+                run(take_root, i - 5)
+                run(square_root, i - 5)
                 run(transpose_x, i - 4)
                 run(transpose_h, i)
-                run(take_root, i - 6)
-                run(square_root, i - 6)
-                run(spread_norm, i - 5)
+                run(spread_norm, i - 4)
+                run(project_first, i - 1)
                 run(correlate, i - 5)
-                run(regroup_x_scalar, i - 4)
+                run(project_second, i - 1)
+                run(regroup_x_vector, i - 4)
                 run(take_stats, i - 2)
                 run(centre, i - 3)
+                run(regroup_x_scalar, i - 4)
                 run(regroup_h, i)
-                run(project, i - 1)
-                run(regroup_x_vector, i - 4)
                 run(finish, i - 6)
                 run(take_moments, i - 2)
                 run(take_abs, i - 5)
-                run_quad(invert_root, i - 3)
-                run_quad(take_norm, i - 3)
-                run(quantise_h, i)

@@ -25,6 +25,7 @@ WORK = 3
 STAT = 8
 RESULTS = 6
 SHARE = 80
+IDLE_COLUMNS = 448
 TINY = 1e-36
 
 FLOPS = 2 * GRAPHS * NODES * F_IN * F_OUT + 2 * GRAPHS * NODES * NODES * F_OUT
@@ -50,6 +51,9 @@ def tile_pearsonattention_pa_t_kernel(tc, h, W_h_words, W_h_scales, beta, out):
 
         ident = const.tile([P, P], F32)
         make_identity(nc, ident[:])
+
+        idle = const.tile([P, IDLE_COLUMNS], BF16)
+        nc.vector.memset(idle[:], 0.0)
 
         w_scales = const.tile([P, F_OUT], U8, align_bytes=64)
         nc.vector.memset(w_scales[:].bitcast(I32), 0)
@@ -100,6 +104,10 @@ def tile_pearsonattention_pa_t_kernel(tc, h, W_h_words, W_h_scales, beta, out):
 
         def transpose_h(pair):
             transposed = ring(psum, 1, pair, [P, PAIR, HALVES, NODES], F32, "h_transposed")
+            nc.tensor.matmul(
+                transposed[:].rearrange("p g u n -> p (g u n)")[:, 0:IDLE_COLUMNS],
+                idle[:, 0:P], idle[:], start=True, stop=True,
+            )
             for g in range(PAIR):
                 words = h_pairs[pair][:, g, :].bitcast(F32)
                 for u in range(HALVES):

@@ -25,6 +25,7 @@ WORK = 3
 STAT = 8
 RESULTS = 6
 SHARE = 80
+LAST = 2
 IDLE_COLUMNS = 448
 TINY = 1e-36
 
@@ -70,6 +71,8 @@ def tile_pearsonattention_pa_t_kernel(tc, h, W_h_words, W_h_scales, beta, out):
             h_pairs[pair] = h_pair
 
         load_h(0)
+        load_h(1)
+        load_h(2)
         for quadrant in range(4):
             nc.sync.dma_start(
                 out=w_scales[32 * quadrant : 32 * quadrant + 4, :].bitcast(I32),
@@ -80,12 +83,14 @@ def tile_pearsonattention_pa_t_kernel(tc, h, W_h_words, W_h_scales, beta, out):
             in_=W_h_words[0].rearrange("p n t -> p (n t)").bitcast(I32),
         )
         nc.sync.dma_start(out=beta_bf16[:], in_=beta.partition_broadcast(P))
-        for pair in range(1, PAIRS):
+        for pair in range(3, PAIRS):
             load_h(pair)
         nc.gpsimd.tensor_copy(out=beta_f32[:], in_=beta_bf16[:])
 
         h_t, h_g, h_q, wh, partials, moments, norms, x_m, x_t, x_g, x_q = {}, {}, {}, {}, {}, {}, {}, {}, {}, {}, {}
-        inv_roots, spread, covs, roots, abs_covs, inv_denoms = {}, {}, {}, {}, {}, {}
+        inv_roots, roots, abs_covs, inv_denoms = {}, {}, {}, {}
+        epilogue = psum.tile([P, 2, PAIR, NODES], F32)
+        spread, cov = epilogue[:, 0, :, :], epilogue[:, 1, :, :]
 
         def new_grouped(kind, pair):
             return ring(sbuf, WORK, pair, [P, PAIR * NODES * 2 * HALVES], BF16, kind + "_grouped", align_bytes=64)
@@ -103,7 +108,7 @@ def tile_pearsonattention_pa_t_kernel(tc, h, W_h_words, W_h_scales, beta, out):
             return codes, scales
 
         def transpose_h(pair):
-            transposed = ring(psum, 1, pair, [P, PAIR, HALVES, NODES], F32, "h_transposed")
+            transposed = ring(psum, 2, pair, [P, PAIR, HALVES, NODES], F32, "h_transposed")
             nc.tensor.matmul(
                 transposed[:].rearrange("p g u n -> p (g u n)")[:, 0:IDLE_COLUMNS],
                 idle[:, 0:P], idle[:], start=True, stop=True,
@@ -189,29 +194,30 @@ def tile_pearsonattention_pa_t_kernel(tc, h, W_h_words, W_h_scales, beta, out):
                     nc.tensor.transpose(transposed[:, g, u, :], words[:, P * u : P * (u + 1)], ident[:])
             x_t[pair] = transposed
 
+        def vector_share(pair):
+            return SHARE if pair < PAIRS - LAST else NODES
+
         def regroup_x_vector(pair):
             x_g[pair] = new_grouped("x", pair)
-            regroup(nc.vector.tensor_copy, x_t[pair], x_g[pair], slice(0, SHARE))
+            regroup(nc.vector.tensor_copy, x_t[pair], x_g[pair], slice(0, vector_share(pair)))
 
         def regroup_x_scalar(pair):
-            regroup(nc.scalar.copy, x_t[pair], x_g[pair], slice(SHARE, NODES))
+            if vector_share(pair) < NODES:
+                regroup(nc.scalar.copy, x_t[pair], x_g[pair], slice(vector_share(pair), NODES))
 
         def quantise_x(pair):
             x_q[pair] = quantise(x_g[pair], "x", pair)
 
         def spread_norm(pair):
-            bank = ring(psum, 1, pair, [P, PAIR, NODES], F32, "spread")
             for g in range(PAIR):
-                nc.tensor.transpose(bank[:, g, :], norms[PAIR * pair + g].to_broadcast([P, P]), ident[:])
-            spread[pair] = bank
+                nc.tensor.transpose(spread[:, g, :], norms[PAIR * pair + g].to_broadcast([P, P]), ident[:])
 
         def correlate(pair):
-            bank = ring(psum, 1, pair, [P, PAIR, NODES], F32, "cov")
             codes, scales = x_q[pair]
             for g in range(PAIR):
                 nodes = slice(NODES * g, NODES * (g + 1))
                 nc.tensor.matmul_mx(
-                    out=bank[:, g, :],
+                    out=cov[:, g, :],
                     lhsT=codes[:, nodes].bitcast(FP8X4),
                     lhsT_scale=scales[:, nodes],
                     rhs=codes[:, nodes].bitcast(FP8X4),
@@ -219,25 +225,24 @@ def tile_pearsonattention_pa_t_kernel(tc, h, W_h_words, W_h_scales, beta, out):
                     start=True,
                     stop=True,
                 )
-            covs[pair] = bank
 
         def take_root(pair):
             root = ring(sbuf, WORK, pair, [P, PAIR, NODES], F32, "root")
             for g in range(PAIR):
                 nc.scalar.activation(
-                    out=root[:, g, :], in_=spread[pair][:, g, :], func=ACT.Abs_reciprocal_sqrt,
+                    out=root[:, g, :], in_=spread[:, g, :], func=ACT.Abs_reciprocal_sqrt,
                     bias=eps[:], scale=norms[PAIR * pair + g],
                 )
             roots[pair] = root
 
         def square_root(pair):
-            inv_denom = ring(sbuf, WORK, pair, [P, PAIR, NODES], F32, "x_grouped", align_bytes=64)
+            inv_denom = ring(sbuf, WORK, pair + 4, [P, PAIR, NODES], F32, "h_grouped", align_bytes=64)
             nc.gpsimd.tensor_tensor(out=inv_denom[:], in0=roots[pair][:], in1=roots[pair][:], op=ALU.mult)
             inv_denoms[pair] = inv_denom
 
         def take_abs(pair):
             abs_cov = ring(sbuf, WORK, pair, [P, PAIR, NODES], F32, "abs_cov")
-            nc.scalar.activation(out=abs_cov[:], in_=covs[pair][:], func=ACT.Abs)
+            nc.scalar.activation(out=abs_cov[:], in_=cov, func=ACT.Abs)
             abs_covs[pair] = abs_cov
 
         def finish(pair):
@@ -262,6 +267,7 @@ def tile_pearsonattention_pa_t_kernel(tc, h, W_h_words, W_h_scales, beta, out):
                 stage(pair // 2)
 
         with tc.manual_schedule():
+            transpose_h(0)
             for i in range(PAIRS + 7):
                 run(quantise_x, i - 5)
                 run(quantise_h, i - 1)
@@ -270,7 +276,7 @@ def tile_pearsonattention_pa_t_kernel(tc, h, W_h_words, W_h_scales, beta, out):
                 run(take_root, i - 5)
                 run(square_root, i - 5)
                 run(transpose_x, i - 4)
-                run(transpose_h, i)
+                run(transpose_h, i + 1)
                 run(spread_norm, i - 4)
                 run(project_first, i - 1)
                 run(correlate, i - 5)

@@ -95,24 +95,33 @@ def tile_pearsonattention_pa_t_kernel(tc, h, W_h_words, W_h_scales, beta, out):
         def new_grouped(kind, pair):
             return ring(sbuf, WORK, pair, [P, PAIR * NODES * 2 * HALVES], BF16, kind + "_grouped", align_bytes=64)
 
-        def regroup(engine_copy, transposed, grouped, nodes):
+        def pieces(pair):
+            return [slice(0, PAIR)] if pair < PAIRS - 1 else [slice(g, g + 1) for g in range(PAIR)]
+
+        def regroup(engine_copy, transposed, grouped, graphs, nodes):
             engine_copy(
-                out=grouped[:].bitcast(F32).rearrange("p (g n u) -> p g n u", g=PAIR, u=HALVES)[:, :, nodes, :],
-                in_=transposed[:].rearrange("p g u n -> p g n u")[:, :, nodes, :],
+                out=grouped[:].bitcast(F32).rearrange("p (g n u) -> p g n u", g=PAIR, u=HALVES)[:, graphs, nodes, :],
+                in_=transposed[:].rearrange("p g u n -> p g n u")[:, graphs, nodes, :],
             )
 
-        def quantise(grouped, kind, pair):
+        def quantise(grouped, kind, pair, groups):
             codes = ring(sbuf, WORK, pair, [P, PAIR * NODES], U32, kind + "_codes", align_bytes=64)
             scales = ring(sbuf, WORK, pair, [P, PAIR * NODES], U8, kind + "_scales", align_bytes=64)
-            nc.vector.quantize_mx(out=codes[:].bitcast(FP8X4), scales=scales[:], in_=grouped[:])
+            for graphs in groups:
+                nodes = slice(NODES * graphs.start, NODES * graphs.stop)
+                values = slice(2 * HALVES * nodes.start, 2 * HALVES * nodes.stop)
+                nc.vector.quantize_mx(
+                    out=codes[:, nodes].bitcast(FP8X4), scales=scales[:, nodes], in_=grouped[:, values],
+                )
             return codes, scales
 
         def transpose_h(pair):
             transposed = ring(psum, 2, pair, [P, PAIR, HALVES, NODES], F32, "h_transposed")
-            nc.tensor.matmul(
-                transposed[:].rearrange("p g u n -> p (g u n)")[:, 0:IDLE_COLUMNS],
-                idle[:, 0:P], idle[:], start=True, stop=True,
-            )
+            if pair == 0 or pair > 2:
+                nc.tensor.matmul(
+                    transposed[:].rearrange("p g u n -> p (g u n)")[:, 0:IDLE_COLUMNS],
+                    idle[:, 0:P], idle[:], start=True, stop=True,
+                )
             for g in range(PAIR):
                 words = h_pairs[pair][:, g, :].bitcast(F32)
                 for u in range(HALVES):
@@ -121,10 +130,10 @@ def tile_pearsonattention_pa_t_kernel(tc, h, W_h_words, W_h_scales, beta, out):
 
         def regroup_h(pair):
             h_g[pair] = new_grouped("h", pair)
-            regroup(nc.scalar.copy, h_t[pair], h_g[pair], slice(0, NODES))
+            regroup(nc.scalar.copy, h_t[pair], h_g[pair], slice(0, PAIR), slice(0, NODES))
 
         def quantise_h(pair):
-            h_q[pair] = quantise(h_g[pair], "h", pair)
+            h_q[pair] = quantise(h_g[pair], "h", pair, [slice(0, PAIR)])
 
         def project(pair, g):
             codes, scales = h_q[pair]
@@ -199,14 +208,15 @@ def tile_pearsonattention_pa_t_kernel(tc, h, W_h_words, W_h_scales, beta, out):
 
         def regroup_x_vector(pair):
             x_g[pair] = new_grouped("x", pair)
-            regroup(nc.vector.tensor_copy, x_t[pair], x_g[pair], slice(0, vector_share(pair)))
+            for graphs in pieces(pair):
+                regroup(nc.vector.tensor_copy, x_t[pair], x_g[pair], graphs, slice(0, vector_share(pair)))
 
         def regroup_x_scalar(pair):
             if vector_share(pair) < NODES:
-                regroup(nc.scalar.copy, x_t[pair], x_g[pair], slice(vector_share(pair), NODES))
+                regroup(nc.scalar.copy, x_t[pair], x_g[pair], slice(0, PAIR), slice(vector_share(pair), NODES))
 
         def quantise_x(pair):
-            x_q[pair] = quantise(x_g[pair], "x", pair)
+            x_q[pair] = quantise(x_g[pair], "x", pair, pieces(pair))
 
         def spread_norm(pair):
             for g in range(PAIR):
@@ -242,21 +252,23 @@ def tile_pearsonattention_pa_t_kernel(tc, h, W_h_words, W_h_scales, beta, out):
 
         def take_abs(pair):
             abs_cov = ring(sbuf, WORK, pair, [P, PAIR, NODES], F32, "abs_cov")
-            nc.scalar.activation(out=abs_cov[:], in_=cov, func=ACT.Abs)
+            for graphs in pieces(pair):
+                nc.scalar.activation(out=abs_cov[:, graphs, :], in_=cov[:, graphs, :], func=ACT.Abs)
             abs_covs[pair] = abs_cov
 
         def finish(pair):
             result = ring(sbuf, RESULTS, pair, [P, PAIR, NODES], F32, "result")
-            nc.vector.scalar_tensor_tensor(
-                out=result[:].rearrange("n g m -> n (g m)"),
-                in0=abs_covs[pair][:].rearrange("n g m -> n (g m)"),
-                scalar=beta_f32[:],
-                in1=inv_denoms[pair][:].rearrange("n g m -> n (g m)"),
-                op0=ALU.mult,
-                op1=ALU.mult,
-            )
-            graphs = out[PAIR * pair : PAIR * (pair + 1)]
-            nc.sync.dma_start(out=graphs.rearrange("b n m -> n b m"), in_=result[:])
+            for graphs in pieces(pair):
+                nc.vector.scalar_tensor_tensor(
+                    out=result[:, graphs, :].rearrange("n g m -> n (g m)"),
+                    in0=abs_covs[pair][:, graphs, :].rearrange("n g m -> n (g m)"),
+                    scalar=beta_f32[:],
+                    in1=inv_denoms[pair][:, graphs, :].rearrange("n g m -> n (g m)"),
+                    op0=ALU.mult,
+                    op1=ALU.mult,
+                )
+                stored = out[PAIR * pair + graphs.start : PAIR * pair + graphs.stop]
+                nc.sync.dma_start(out=stored.rearrange("b n m -> n b m"), in_=result[:, graphs, :])
 
         def run(stage, pair):
             if 0 <= pair < PAIRS:
@@ -273,7 +285,6 @@ def tile_pearsonattention_pa_t_kernel(tc, h, W_h_words, W_h_scales, beta, out):
                 run(quantise_h, i - 1)
                 run_quad(invert_root, i - 3)
                 run_quad(take_norm, i - 3)
-                run(take_root, i - 5)
                 run(square_root, i - 5)
                 run(transpose_x, i - 4)
                 run(transpose_h, i + 1)
@@ -288,4 +299,5 @@ def tile_pearsonattention_pa_t_kernel(tc, h, W_h_words, W_h_scales, beta, out):
                 run(regroup_h, i)
                 run(finish, i - 6)
                 run(take_moments, i - 2)
+                run(take_root, i - 4)
                 run(take_abs, i - 5)

from contextlib import ExitStack

import concourse.mybir as mybir
from concourse.masks import make_identity

F32 = mybir.dt.float32
BF16 = mybir.dt.bfloat16
I32 = mybir.dt.int32
U32 = mybir.dt.uint32
U8 = mybir.dt.uint8
FP8X4 = mybir.dt.float8_e4m3fn_x4
ACT = mybir.ActivationFunctionType
ALU = mybir.AluOpType

P = 128
GRAPHS = 64
NODES = 128
F_IN = 512
F_OUT = 512
HALVES = 2
PAIR = 2
PAIRS = GRAPHS // PAIR
EPS = 1e-8
WORK = 3
STAT = 8
RESULTS = 6
SHARE = 80
LAST = 2
IDLE_COLUMNS = 448
TINY = 1e-36

FLOPS = 2 * GRAPHS * NODES * F_IN * F_OUT + 2 * GRAPHS * NODES * NODES * F_OUT


def tile_pearsonattention_pa_t_kernel(tc, h, W_h_words, W_h_scales, beta, out):
    nc = tc.nc
    with ExitStack() as ctx:
        const = ctx.enter_context(tc.tile_pool(name="const", bufs=1))
        h_pool = ctx.enter_context(tc.tile_pool(name="h_pool", bufs=PAIRS))
        sbuf = ctx.enter_context(tc.tile_pool(name="sbuf", bufs=1))
        psum = ctx.enter_context(tc.psum_pool(name="psum", bufs=1))

        def ring(pool, depth, index, shape, dtype, name, **how):
            return pool.tile(shape, dtype, name=name, tag="%s_%d" % (name, index % depth), **how)

        eps = const.tile([P, 1], F32)
        nc.vector.memset(eps[:], EPS)
        tiny = const.tile([P, 1], F32)
        nc.vector.memset(tiny[:], TINY)
        warm = const.tile([P, 1], F32)
        nc.scalar.activation(out=warm[:], in_=eps[:], func=ACT.Abs_reciprocal_sqrt)

        ident = const.tile([P, P], F32)
        make_identity(nc, ident[:])

        idle = const.tile([P, IDLE_COLUMNS], BF16)
        nc.vector.memset(idle[:], 0.0)

        w_scales = const.tile([P, F_OUT], U8, align_bytes=64)
        nc.vector.memset(w_scales[:].bitcast(I32), 0)
        w_codes = const.tile([P, F_OUT], U32, align_bytes=64)
        beta_bf16 = const.tile([P, 1], BF16)
        beta_f32 = const.tile([P, 1], F32)

        h_pairs = {}

        def load_h(pair):
            h_pair = h_pool.tile([P, PAIR, F_IN], BF16)
            graphs = h[PAIR * pair : PAIR * (pair + 1)]
            nc.sync.dma_start(out=h_pair[:], in_=graphs.rearrange("b n f -> n b f"))
            h_pairs[pair] = h_pair

        load_h(0)
        load_h(1)
        load_h(2)
        for quadrant in range(4):
            nc.sync.dma_start(
                out=w_scales[32 * quadrant : 32 * quadrant + 4, :].bitcast(I32),
                in_=W_h_scales[0, 4 * quadrant : 4 * quadrant + 4, :].bitcast(I32),
            )
        nc.sync.dma_start(
            out=w_codes[:].bitcast(I32),
            in_=W_h_words[0].rearrange("p n t -> p (n t)").bitcast(I32),
        )
        nc.sync.dma_start(out=beta_bf16[:], in_=beta.partition_broadcast(P))
        for pair in range(3, PAIRS):
            load_h(pair)
        nc.gpsimd.tensor_copy(out=beta_f32[:], in_=beta_bf16[:])

        h_t, h_g, h_q, wh, partials, moments, norms, x_m, x_t, x_g, x_q = {}, {}, {}, {}, {}, {}, {}, {}, {}, {}, {}
        inv_roots, roots, abs_covs, inv_denoms = {}, {}, {}, {}
        epilogue = psum.tile([P, 2, PAIR, NODES], F32)
        spread, cov = epilogue[:, 0, :, :], epilogue[:, 1, :, :]

        def new_grouped(kind, pair):
            return ring(sbuf, WORK, pair, [P, PAIR * NODES * 2 * HALVES], BF16, kind + "_grouped", align_bytes=64)

        def pieces(pair):
            return [slice(0, PAIR)] if pair < PAIRS - 1 else [slice(g, g + 1) for g in range(PAIR)]

        def regroup(engine_copy, transposed, grouped, graphs, nodes):
            engine_copy(
                out=grouped[:].bitcast(F32).rearrange("p (g n u) -> p g n u", g=PAIR, u=HALVES)[:, graphs, nodes, :],
                in_=transposed[:].rearrange("p g u n -> p g n u")[:, graphs, nodes, :],
            )

        def quantise(grouped, kind, pair, groups):
            codes = ring(sbuf, WORK, pair, [P, PAIR * NODES], U32, kind + "_codes", align_bytes=64)
            scales = ring(sbuf, WORK, pair, [P, PAIR * NODES], U8, kind + "_scales", align_bytes=64)
            for graphs in groups:
                nodes = slice(NODES * graphs.start, NODES * graphs.stop)
                values = slice(2 * HALVES * nodes.start, 2 * HALVES * nodes.stop)
                nc.vector.quantize_mx(
                    out=codes[:, nodes].bitcast(FP8X4), scales=scales[:, nodes], in_=grouped[:, values],
                )
            return codes, scales

        def transpose_h(pair):
            transposed = ring(psum, 2, pair, [P, PAIR, HALVES, NODES], F32, "h_transposed")
            if pair == 0 or pair > 2:
                nc.tensor.matmul(
                    transposed[:].rearrange("p g u n -> p (g u n)")[:, 0:IDLE_COLUMNS],
                    idle[:, 0:P], idle[:], start=True, stop=True,
                )
            for g in range(PAIR):
                words = h_pairs[pair][:, g, :].bitcast(F32)
                for u in range(HALVES):
                    nc.tensor.transpose(transposed[:, g, u, :], words[:, u : F_IN // 2 : HALVES], ident[:])
            h_t[pair] = transposed

        def regroup_h(pair):
            h_g[pair] = new_grouped("h", pair)
            regroup(nc.scalar.copy, h_t[pair], h_g[pair], slice(0, PAIR), slice(0, NODES))

        def quantise_h(pair):
            h_q[pair] = quantise(h_g[pair], "h", pair, [slice(0, PAIR)])

        def project(pair, g):
            codes, scales = h_q[pair]
            nodes = slice(NODES * g, NODES * (g + 1))
            acc = ring(psum, 2 * PAIR, PAIR * pair + g, [P, F_OUT], F32, "wh_acc")
            nc.tensor.matmul_mx(
                out=acc[:],
                lhsT=codes[:, nodes].bitcast(FP8X4),
                lhsT_scale=scales[:, nodes],
                rhs=w_codes[:].bitcast(FP8X4),
                rhs_scale=w_scales[:],
                start=True,
                stop=True,
            )
            wh[(pair, g)] = acc

        def project_first(pair):
            project(pair, 0)

        def project_second(pair):
            project(pair, 1)

        def take_stats(pair):
            for g in range(PAIR):
                partial = ring(sbuf, STAT, PAIR * pair + g, [P, 6], F32, "partial")
                nc.vector.bn_stats(out=partial[:], in_=wh[(pair, g)][:])
                partials[(pair, g)] = partial

        def take_moments(pair):
            quad, half = divmod(pair, 2)
            if half == 0:
                moments[quad] = ring(sbuf, STAT, quad, [P, 2 * PAIR, 2], F32, "mean_var")
            for g in range(PAIR):
                nc.vector.bn_aggr(out=moments[quad][:, PAIR * half + g, :], in_=partials[(pair, g)][:])

        def invert_root(quad):
            inv_root = ring(sbuf, STAT, quad, [P, 2 * PAIR], F32, "inv_root")
            nc.scalar.activation(
                out=inv_root[:], in_=moments[quad][:, :, 1], func=ACT.Abs_reciprocal_sqrt,
                bias=tiny[:], scale=1.0 / F_OUT,
            )
            inv_roots[quad] = inv_root

        def take_norm(quad):
            norm = ring(sbuf, STAT, quad, [P, 2 * PAIR], F32, "norm")
            nc.gpsimd.tensor_tensor(out=norm[:], in0=moments[quad][:, :, 1], in1=inv_roots[quad][:], op=ALU.mult)
            for g in range(2 * PAIR):
                norms[2 * PAIR * quad + g] = norm[:, g : g + 1]

        def centre(pair):
            neg_centred = ring(sbuf, WORK, pair, [P, PAIR, F_OUT], BF16, "neg_centred")
            for g in range(PAIR):
                nc.scalar.activation(
                    out=neg_centred[:, g, :].rearrange("n (u p e) -> n u p e", u=HALVES, e=2),
                    in_=wh[(pair, g)][:].rearrange("n (p u e) -> n u p e", u=HALVES, e=2),
                    func=ACT.Identity,
                    bias=moments[pair // 2][:, PAIR * (pair % 2) + g, 0:1],
                    scale=-1.0,
                )
            x_m[pair] = neg_centred

        def transpose_x(pair):
            transposed = ring(psum, 1, pair, [P, PAIR, HALVES, NODES], F32, "x_transposed")
            for g in range(PAIR):
                words = x_m[pair][:, g, :].bitcast(F32)
                for u in range(HALVES):
                    nc.tensor.transpose(transposed[:, g, u, :], words[:, P * u : P * (u + 1)], ident[:])
            x_t[pair] = transposed

        def vector_share(pair):
            return SHARE if pair < PAIRS - LAST else NODES

        def regroup_x_vector(pair):
            x_g[pair] = new_grouped("x", pair)
            for graphs in pieces(pair):
                regroup(nc.vector.tensor_copy, x_t[pair], x_g[pair], graphs, slice(0, vector_share(pair)))

        def regroup_x_scalar(pair):
            if vector_share(pair) < NODES:
                regroup(nc.scalar.copy, x_t[pair], x_g[pair], slice(0, PAIR), slice(vector_share(pair), NODES))

        def quantise_x(pair):
            x_q[pair] = quantise(x_g[pair], "x", pair, pieces(pair))

        def spread_norm(pair):
            for g in range(PAIR):
                nc.tensor.transpose(spread[:, g, :], norms[PAIR * pair + g].to_broadcast([P, P]), ident[:])

        def correlate(pair):
            codes, scales = x_q[pair]
            for g in range(PAIR):
                nodes = slice(NODES * g, NODES * (g + 1))
                nc.tensor.matmul_mx(
                    out=cov[:, g, :],
                    lhsT=codes[:, nodes].bitcast(FP8X4),
                    lhsT_scale=scales[:, nodes],
                    rhs=codes[:, nodes].bitcast(FP8X4),
                    rhs_scale=scales[:, nodes],
                    start=True,
                    stop=True,
                )

        def take_root(pair):
            root = ring(sbuf, WORK, pair, [P, PAIR, NODES], F32, "root")
            for g in range(PAIR):
                nc.scalar.activation(
                    out=root[:, g, :], in_=spread[:, g, :], func=ACT.Abs_reciprocal_sqrt,
                    bias=eps[:], scale=norms[PAIR * pair + g],
                )
            roots[pair] = root

        def square_root(pair):
            inv_denom = ring(sbuf, WORK, pair + 4, [P, PAIR, NODES], F32, "h_grouped", align_bytes=64)
            nc.gpsimd.tensor_tensor(out=inv_denom[:], in0=roots[pair][:], in1=roots[pair][:], op=ALU.mult)
            inv_denoms[pair] = inv_denom

        def take_abs(pair):
            abs_cov = ring(sbuf, WORK, pair, [P, PAIR, NODES], F32, "abs_cov")
            for graphs in pieces(pair):
                nc.scalar.activation(out=abs_cov[:, graphs, :], in_=cov[:, graphs, :], func=ACT.Abs)
            abs_covs[pair] = abs_cov

        def finish(pair):
            result = ring(sbuf, RESULTS, pair, [P, PAIR, NODES], F32, "result")
            for graphs in pieces(pair):
                nc.vector.scalar_tensor_tensor(
                    out=result[:, graphs, :].rearrange("n g m -> n (g m)"),
                    in0=abs_covs[pair][:, graphs, :].rearrange("n g m -> n (g m)"),
                    scalar=beta_f32[:],
                    in1=inv_denoms[pair][:, graphs, :].rearrange("n g m -> n (g m)"),
                    op0=ALU.mult,
                    op1=ALU.mult,
                )
                stored = out[PAIR * pair + graphs.start : PAIR * pair + graphs.stop]
                nc.sync.dma_start(out=stored.rearrange("b n m -> n b m"), in_=result[:, graphs, :])

        def run(stage, pair):
            if 0 <= pair < PAIRS:
                stage(pair)

        def run_quad(stage, pair):
            if 0 <= pair < PAIRS and pair % 2 == 1:
                stage(pair // 2)

        with tc.manual_schedule():
            transpose_h(0)
            for i in range(PAIRS + 7):
                run(quantise_x, i - 5)
                run(quantise_h, i - 1)
                run_quad(invert_root, i - 3)
                run_quad(take_norm, i - 3)
                run(square_root, i - 5)
                run(transpose_x, i - 4)
                run(transpose_h, i + 1)
                run(spread_norm, i - 4)
                run(project_first, i - 1)
                run(correlate, i - 5)
                run(project_second, i - 1)
                run(regroup_x_vector, i - 4)
                run(take_stats, i - 2)
                run(centre, i - 3)
                run(regroup_x_scalar, i - 4)
                run(regroup_h, i)
                run(finish, i - 6)
                run(take_moments, i - 2)
                run(take_root, i - 4)
                run(take_abs, i - 5)
